import numpy as np
import ml_dtypes


def mxq(x, axis, fmt="e4m3"):
    dtype, down = {"e4m3": (ml_dtypes.float8_e4m3fn, 7), "e5m2": (ml_dtypes.float8_e5m2, 14)}[fmt]
    v = np.moveaxis(np.asarray(x, np.float32).astype(ml_dtypes.bfloat16).astype(np.float64), axis, -1)
    blocks = v.reshape(v.shape[:-1] + (-1, 32))
    amax = np.abs(blocks).max(-1, keepdims=True)
    byte = np.maximum(np.where(amax > 0, np.frexp(amax)[1] - 1 + 127, 0) - down, 1)
    scale = np.exp2(byte - 127.0)
    codes = (blocks / scale).astype(np.float32).astype(dtype).astype(np.float64)
    return np.moveaxis((codes * scale).reshape(v.shape), -1, axis)


WIDE = False


def mx_kscale(k):
    if not WIDE:
        return np.ones(k)
    levels = np.array([10, -10, 5, -5, 0])
    a = np.random.permutation(np.resize(levels, k // 512 * 4)).reshape(k // 512, 4)
    idx = np.arange(k)
    return np.exp2(a[idx // 512, idx % 128 // 32])


BF16 = ml_dtypes.bfloat16


def bf(x):
    return np.asarray(x, np.float32).astype(BF16)


def f64(x):
    return np.asarray(x).astype(np.float64)


E2M1 = np.array([0.0, 0.5, 1.0, 1.5, 2.0, 3.0, 4.0, 6.0, -0.0, -0.5, -1.0, -1.5, -2.0, -3.0, -4.0, -6.0])


def pack_weight(w, fmt):
    k, n = w.shape
    w = f64(bf(w)).reshape(k // 32, 32, n)
    amax = np.abs(w).max(1)
    if fmt == "e4m3":
        byte = np.frexp(amax)[1] - 1 + 127 - 7
    else:
        mant, ex = np.frexp(amax / 6.0)
        byte = np.where(mant > 0.5, ex, ex - 1) + 127
    byte = np.clip(np.where(amax > 0, byte, 1), 1, 254)
    scaled = (w * np.exp2(127.0 - byte)[:, None, :]).reshape(k, n).astype(np.float32)
    by_word = np.ascontiguousarray(scaled.reshape(k // 512, 128, 4, n).transpose(0, 1, 3, 2))
    if fmt == "e4m3":
        words = by_word.astype(ml_dtypes.float8_e4m3fn).view(np.uint8)
    else:
        c = by_word.astype(ml_dtypes.float4_e2m1fn).view(np.uint8) & 0xF
        words = c[..., 0::2] | (c[..., 1::2] << 4)
    return np.ascontiguousarray(words), np.ascontiguousarray(byte.astype(np.uint8).reshape(k // 512, 16, n))


def unpack_weight(words, scales, fmt):
    g, p, n, _ = words.shape
    if fmt == "e4m3":
        vals = np.ascontiguousarray(words).view(ml_dtypes.float8_e4m3fn).astype(np.float64)
    else:
        nib = np.empty((g, p, n, 4), np.uint8)
        nib[..., 0::2] = words & 0xF
        nib[..., 1::2] = words >> 4
        vals = E2M1[nib]
    vals = vals * np.repeat(np.exp2(scales.astype(np.float64) - 127.0), 8, axis=1)[..., None]
    return vals.transpose(0, 1, 3, 2).reshape(g * 512, n)


B, I, H = 128, 16384, 256
EPS = 1e-5


def sigmoid(v):
    return 1.0 / (1.0 + np.exp(-v))


def _bn(v, gamma, beta):
    m = np.mean(v, axis=0)
    var = np.var(v, axis=0)
    return (v - m) * (gamma / np.sqrt(var + EPS)) + beta


def setup_inputs():
    rn = np.random.standard_normal
    s = mx_kscale(I)
    x = bf(rn((B, I)) * s)
    c = bf(rn((B, H)))
    h = bf(rn((B, H)))
    w_ih_words, w_ih_scales = pack_weight((rn((4 * H, I)) / np.sqrt(I) / s).T, "e4m3")
    return {"x": x,
            "c": c,
            "h": h,
            "w_ih_words": w_ih_words,
            "w_ih_scales": w_ih_scales,
            "w_hh": bf(rn((4 * H, H)) / np.sqrt(H)),
            "b": bf(0.3 * rn(4 * H)),
            "g_ih": bf(1.0 + 0.1 * rn(4 * H)),
            "b_ih": bf(0.3 * rn(4 * H)),
            "g_hh": bf(1.0 + 0.1 * rn(4 * H)),
            "b_hh": bf(0.3 * rn(4 * H)),
            "g_c": bf(1.0 + 0.1 * rn(H)),
            "b_c": bf(0.3 * rn(H))}


def reference(x, c, h, w_ih_words, w_ih_scales, w_hh, b, g_ih, b_ih, g_hh, b_hh, g_c, b_c):
    ih = mxq(f64(x), 1, "e4m3") @ unpack_weight(w_ih_words, w_ih_scales, "e4m3")
    hh = f64(h) @ f64(w_hh).T
    ih = _bn(ih, f64(g_ih), f64(b_ih))
    hh = _bn(hh, f64(g_hh), f64(b_hh))
    gates = ih + hh + f64(b)
    f, i, o, g = np.split(gates, 4, axis=1)
    f = sigmoid(f)
    i = sigmoid(i)
    o = sigmoid(o)
    g = np.tanh(g)
    c_next = f * f64(c) + i * g
    c_next = _bn(c_next, f64(g_c), f64(b_c))
    h_next = o * np.tanh(c_next)
    return (c_next, h_next)

@@ -1,0 +1,317 @@
+from contextlib import ExitStack
+
+import concourse.mybir as mybir
+from concourse.masks import make_identity
+
+F32 = mybir.dt.float32
+BF16 = mybir.dt.bfloat16
+I32 = mybir.dt.int32
+U32 = mybir.dt.uint32
+U8 = mybir.dt.uint8
+FP8X4 = mybir.dt.float8_e4m3fn_x4
+ALU = mybir.AluOpType
+ACT = mybir.ActivationFunctionType
+
+P = 128
+BATCH = 128
+IN = 16384
+HID = 256
+GATES = 4 * HID
+EPS = 1e-5
+
+K_PASS = 512
+PASSES = IN // K_PASS
+TILES = GATES // P
+HALVES = HID // P
+
+X_CHUNK_PASSES = 4
+X_CHUNKS = PASSES // X_CHUNK_PASSES
+PLANES_PER_TILE = 4
+
+FORGET, IN_GATE, OUT_GATE, CELL = 0, 1, 2, 3
+
+COL_B, COL_G_IH, COL_B_IH, COL_G_HH, COL_B_HH = 0, 8, 16, 24, 32
+COL_G_C, COL_B_C = 40, 42
+VECTOR_COLS = 44
+
+FLOPS = 2 * BATCH * IN * GATES + 2 * BATCH * HID * GATES
+
+
+def batch_norm_scale(nc, pool, neg_half, sources, gamma, label):
+    count = len(sources)
+    stats = pool.tile([P, count, 6], F32, name=label + "_stats")
+    mean_var = pool.tile([P, count, 2], F32, name=label + "_mean_var")
+    for t in range(count):
+        nc.vector.bn_stats(out=stats[:, t, :], in_=sources[t])
+    for t in range(count):
+        nc.vector.bn_aggr(out=mean_var[:, t, :], in_=stats[:, t, :])
+    var_eps = pool.tile([P, count], F32, name=label + "_var_eps")
+    nc.vector.tensor_scalar_add(out=var_eps[:], in0=mean_var[:, :, 1], scalar1=EPS)
+    rstd = pool.tile([P, count], F32, name=label + "_rstd")
+    nc.gpsimd.tensor_tensor(out=rstd[:], in0=var_eps[:], in1=neg_half[:, 0:count], op=ALU.pow)
+    scale = pool.tile([P, count], F32, name=label + "_scale")
+    nc.vector.tensor_mul(out=scale[:], in0=rstd[:], in1=gamma)
+    shift = pool.tile([P, count], F32, name=label + "_shift")
+    nc.vector.scalar_tensor_tensor(
+        out=shift[:], in0=mean_var[:, :, 0], scalar=-1.0, in1=scale[:], op0=ALU.mult, op1=ALU.mult
+    )
+    return scale, shift
+
+
+def tile_lstmcell_k_kernel(
+    tc, x, c, h, w_ih_words, w_ih_scales, w_hh, b, g_ih, b_ih, g_hh, b_hh, g_c, b_c, out_0, out_1
+):
+    nc = tc.nc
+    with ExitStack() as whole:
+        keep = whole.enter_context(tc.tile_pool(name="keep", bufs=1))
+        w_pool = whole.enter_context(tc.tile_pool(name="w_words", bufs=PASSES))
+
+        w_planes = keep.tile([P, PASSES // PLANES_PER_TILE, GATES], U8, align_bytes=64)
+        nc.vector.memset(w_planes[:].bitcast(I32), 0)
+        vector_rows = keep.tile([P, P], BF16)
+        nc.vector.memset(vector_rows[:], 0.0)
+        neg_half = keep.tile([P, TILES], F32)
+        nc.vector.memset(neg_half[:], -0.5)
+        ident_f32 = keep.tile([P, P], F32)
+        make_identity(nc, ident_f32[:])
+        ident_bf16 = keep.tile([P, P], BF16)
+        nc.vector.tensor_copy(out=ident_bf16[:], in_=ident_f32[:])
+        table_in = keep.tile([P, 1], F32)
+        nc.vector.memset(table_in[:], 0.0)
+        table_out = keep.tile([P, 1], F32)
+        nc.scalar.activation(out=table_out[:], in_=table_in[:], func=ACT.Sigmoid)
+
+        with ExitStack() as head:
+            stage = head.enter_context(tc.tile_pool(name="stage", bufs=1))
+            x_pool = head.enter_context(tc.tile_pool(name="x", bufs=X_CHUNKS))
+            grouped_pool = head.enter_context(tc.tile_pool(name="grouped", bufs=3))
+
+            w_hh_rows = stage.tile([P, TILES, HID], BF16)
+            nc.sync.dma_start(out=w_hh_rows[:], in_=w_hh.rearrange("(j p) k -> p j k", p=P))
+            x_chunks = []
+            chunk_cols = X_CHUNK_PASSES * K_PASS
+            for i in range(X_CHUNKS):
+                x_chunk = x_pool.tile([P, chunk_cols], BF16)
+                nc.sync.dma_start(out=x_chunk[:], in_=x[:, i * chunk_cols : (i + 1) * chunk_cols])
+                x_chunks.append(x_chunk)
+
+            h_rows = stage.tile([P, HID], BF16)
+            nc.scalar.dma_start(out=h_rows[:], in_=h[:, :])
+            c_rows = stage.tile([P, HID], BF16)
+            nc.scalar.dma_start(out=c_rows[:], in_=c[:, :])
+            for col, vector in (
+                (COL_B, b),
+                (COL_G_IH, g_ih),
+                (COL_B_IH, b_ih),
+                (COL_G_HH, g_hh),
+                (COL_B_HH, b_hh),
+                (COL_G_C, g_c),
+                (COL_B_C, b_c),
+            ):
+                rows = vector.shape[0] // P
+                nc.scalar.dma_start(
+                    out=vector_rows[col : col + rows, :], in_=vector.rearrange("(r e) -> r e", e=P)
+                )
+
+            for m in range(PASSES // PLANES_PER_TILE):
+                for quad in range(4):
+                    nc.sync.dma_start(
+                        out=w_planes[32 * quad : 32 * quad + 16, m, :].bitcast(I32),
+                        in_=w_ih_scales[
+                            PLANES_PER_TILE * m : PLANES_PER_TILE * (m + 1), 4 * quad : 4 * quad + 4, :
+                        ].bitcast(I32),
+                    )
+
+            w_words = []
+            for g in range(PASSES):
+                words = w_pool.tile([P, GATES], U32, align_bytes=64)
+                nc.sync.dma_start(
+                    out=words[:].bitcast(I32),
+                    in_=w_ih_words[g].rearrange("p n t -> p (n t)").bitcast(I32),
+                )
+                w_words.append(words)
+
+            head_psum = head.enter_context(tc.psum_pool(name="head_psum", bufs=1))
+            hh_psum = head.enter_context(tc.psum_pool(name="hh_psum", bufs=2))
+            x_psum = head.enter_context(tc.psum_pool(name="x_psum", bufs=4))
+
+            small_t = head_psum.tile([P, 2 * HALVES + 1, P], BF16)
+            h_t = stage.tile([P, HALVES, BATCH], BF16)
+            c_t = keep.tile([P, HALVES, BATCH], BF16)
+            vectors = keep.tile([P, VECTOR_COLS], F32)
+            for s in range(HALVES):
+                nc.tensor.transpose(small_t[:, s, :], h_rows[:, s * P : (s + 1) * P], ident_bf16[:])
+            nc.vector.tensor_copy(out=h_t[:], in_=small_t[:, 0:HALVES, :])
+            for s in range(HALVES):
+                nc.tensor.transpose(
+                    small_t[:, HALVES + s, :], c_rows[:, s * P : (s + 1) * P], ident_bf16[:]
+                )
+            nc.vector.tensor_copy(out=c_t[:], in_=small_t[:, HALVES : 2 * HALVES, :])
+            nc.tensor.transpose(small_t[:, 2 * HALVES, :], vector_rows[:], ident_bf16[:])
+            nc.vector.tensor_copy(out=vectors[:], in_=small_t[:, 2 * HALVES, 0:VECTOR_COLS])
+
+            w_hh_t = stage.tile([P, HALVES, GATES], BF16)
+            for s in range(HALVES):
+                w_hh_bank = hh_psum.tile([P, TILES, P], BF16, tag="hh")
+                for j in range(TILES):
+                    nc.tensor.transpose(
+                        w_hh_bank[:, j, :], w_hh_rows[:, j, s * P : (s + 1) * P], ident_bf16[:]
+                    )
+                nc.scalar.copy(
+                    out=w_hh_t[:, s, :].rearrange("p (j n) -> p j n", j=TILES), in_=w_hh_bank[:]
+                )
+            tiles_per_bank = 4
+            hh_tiles = []
+            for bank in range(TILES // tiles_per_bank):
+                hh_bank = hh_psum.tile([P, tiles_per_bank, BATCH], F32, tag="hh")
+                for t in range(tiles_per_bank):
+                    j = bank * tiles_per_bank + t
+                    for s in range(HALVES):
+                        nc.tensor.matmul(
+                            hh_bank[:, t, :],
+                            lhsT=w_hh_t[:, s, j * P : (j + 1) * P],
+                            rhs=h_t[:, s, :],
+                            start=(s == 0),
+                            stop=(s == HALVES - 1),
+                        )
+                    hh_tiles.append(hh_bank[:, t, :])
+            hh_scale, hh_shift = batch_norm_scale(
+                nc, stage, neg_half, hh_tiles, vectors[:, COL_G_HH : COL_G_HH + TILES], "hh"
+            )
+            for col in (COL_B, COL_B_IH, COL_B_HH):
+                nc.vector.tensor_add(out=hh_shift[:], in0=hh_shift[:], in1=vectors[:, col : col + TILES])
+            hh_part = keep.tile([P, TILES, BATCH], F32)
+            for j in range(TILES):
+                nc.scalar.activation(
+                    out=hh_part[:, j, :],
+                    in_=hh_tiles[j],
+                    func=ACT.Identity,
+                    scale=hh_scale[:, j : j + 1],
+                    bias=hh_shift[:, j : j + 1],
+                )
+
+            x_words = keep.tile([P, PASSES, BATCH], U32, align_bytes=64)
+            x_planes = keep.tile([P, PASSES, BATCH], U8, align_bytes=64)
+            passes_per_bank = 2
+            for i in range(X_CHUNKS):
+                pairs = x_chunks[i][:].bitcast(F32)
+                grouped = grouped_pool.tile([P, X_CHUNK_PASSES, BATCH, 4], BF16, align_bytes=64)
+                for first in range(0, X_CHUNK_PASSES, passes_per_bank):
+                    x_bank = x_psum.tile([P, passes_per_bank, 2, BATCH], F32)
+                    for r in range(passes_per_bank):
+                        start_word = (first + r) * (K_PASS // 2)
+                        for u in range(2):
+                            nc.tensor.transpose(
+                                x_bank[:, r, u, :],
+                                pairs[:, start_word + u : start_word + K_PASS // 2 : 2],
+                                ident_f32[:],
+                            )
+                    nc.scalar.copy(
+                        out=grouped[:].bitcast(F32)[:, first : first + passes_per_bank, :, :],
+                        in_=x_bank[:].rearrange("p r u b -> p r b u"),
+                    )
+                chunk = slice(i * X_CHUNK_PASSES, (i + 1) * X_CHUNK_PASSES)
+                nc.vector.quantize_mx(
+                    out=x_words[:, chunk, :].rearrange("p g b -> p (g b)").bitcast(FP8X4),
+                    scales=x_planes[:, chunk, :].rearrange("p g b -> p (g b)"),
+                    in_=grouped[:].rearrange("p g b t -> p (g b t)"),
+                )
+
+        acc_pool = whole.enter_context(tc.psum_pool(name="acc", bufs=1))
+        tail = whole.enter_context(tc.tile_pool(name="tail", bufs=1))
+        acc = [acc_pool.tile([P, BATCH], F32, name="acc%d" % j) for j in range(TILES)]
+        for g in range(PASSES):
+            first_row = 4 * (g % PLANES_PER_TILE)
+            for j in range(TILES):
+                cols = slice(j * P, (j + 1) * P)
+                nc.tensor.matmul_mx(
+                    out=acc[j][:],
+                    lhsT=w_words[g][:, cols].bitcast(FP8X4),
+                    lhsT_scale=w_planes[first_row:P, g // PLANES_PER_TILE, cols],
+                    rhs=x_words[:, g, :].bitcast(FP8X4),
+                    rhs_scale=x_planes[:, g, :],
+                    start=(g == 0),
+                    stop=(g == PASSES - 1),
+                )
+
+        gate_sum = tail.tile([P, TILES, BATCH], F32)
+        gate = tail.tile([P, TILES, BATCH], F32)
+
+        def finish_gates(first_gate, gate_count, label):
+            tiles = range(first_gate * HALVES, (first_gate + gate_count) * HALVES)
+            scale, shift = batch_norm_scale(
+                nc,
+                tail,
+                neg_half,
+                [acc[j][:] for j in tiles],
+                vectors[:, COL_G_IH + tiles[0] : COL_G_IH + tiles[0] + len(tiles)],
+                label,
+            )
+            for t, j in enumerate(tiles):
+                nc.vector.scalar_tensor_tensor(
+                    out=gate_sum[:, j, :],
+                    in0=acc[j][:],
+                    scalar=scale[:, t : t + 1],
+                    in1=hh_part[:, j, :],
+                    op0=ALU.mult,
+                    op1=ALU.add,
+                )
+                nc.scalar.activation(
+                    out=gate[:, j, :],
+                    in_=gate_sum[:, j, :],
+                    func=ACT.Tanh if j // HALVES == CELL else ACT.Sigmoid,
+                    bias=shift[:, t : t + 1],
+                )
+
+        def gate_tiles(which):
+            return gate[:, which * HALVES : (which + 1) * HALVES, :]
+
+        finish_gates(FORGET, 2, "forget_in")
+        finish_gates(CELL, 1, "cell")
+        finish_gates(OUT_GATE, 1, "out")
+
+        kept = tail.tile([P, HALVES, BATCH], F32)
+        nc.vector.tensor_mul(out=kept[:], in0=gate_tiles(FORGET), in1=c_t[:])
+        added = tail.tile([P, HALVES, BATCH], F32)
+        nc.vector.tensor_mul(out=added[:], in0=gate_tiles(IN_GATE), in1=gate_tiles(CELL))
+        c_raw = tail.tile([P, HALVES, BATCH], F32)
+        nc.vector.tensor_add(out=c_raw[:], in0=kept[:], in1=added[:])
+        c_scale, c_shift = batch_norm_scale(
+            nc,
+            tail,
+            neg_half,
+            [c_raw[:, s, :] for s in range(HALVES)],
+            vectors[:, COL_G_C : COL_G_C + HALVES],
+            "c",
+        )
+        nc.vector.tensor_add(
+            out=c_shift[:], in0=c_shift[:], in1=vectors[:, COL_B_C : COL_B_C + HALVES]
+        )
+        c_next_t = tail.tile([P, HALVES, BATCH], F32)
+        tanh_c = tail.tile([P, HALVES, BATCH], F32)
+        for s in range(HALVES):
+            nc.vector.tensor_scalar(
+                out=c_next_t[:, s, :],
+                in0=c_raw[:, s, :],
+                scalar1=c_scale[:, s : s + 1],
+                scalar2=c_shift[:, s : s + 1],
+                op0=ALU.mult,
+                op1=ALU.add,
+            )
+            nc.scalar.activation(
+                out=tanh_c[:, s, :],
+                in_=c_raw[:, s, :],
+                func=ACT.Tanh,
+                scale=c_scale[:, s : s + 1],
+                bias=c_shift[:, s : s + 1],
+            )
+        h_next_t = tail.tile([P, HALVES, BATCH], F32)
+        nc.vector.tensor_mul(out=h_next_t[:], in0=gate_tiles(OUT_GATE), in1=tanh_c[:])
+
+        for result_t, out, bank_tag in ((c_next_t, out_0, "acc0"), (h_next_t, out_1, "acc1")):
+            result_bank = acc_pool.tile([P, HALVES, P], F32, tag=bank_tag, name="t_" + bank_tag)
+            for s in range(HALVES):
+                nc.tensor.transpose(result_bank[:, s, :], result_t[:, s, :], ident_f32[:])
+            result = tail.tile([P, HID], F32, name="r_" + bank_tag)
+            nc.scalar.copy(out=result[:].rearrange("p (s n) -> p s n", s=HALVES), in_=result_bank[:])
+            nc.sync.dma_start(out=out[:, :], in_=result[:])

@@ -21,14 +21,16 @@ EPS = 1e-5
 
 K_PASS = 512
 PASSES = IN // K_PASS
+BLOCK_PASSES = 4
+BLOCKS = PASSES // BLOCK_PASSES
+LATE_BLOCKS = 6
+EARLY_BLOCKS = BLOCKS - LATE_BLOCKS
+
 TILES = GATES // P
 HALVES = HID // P
-
-X_CHUNK_PASSES = 4
-X_CHUNKS = PASSES // X_CHUNK_PASSES
-PLANES_PER_TILE = 4
-
-FORGET, IN_GATE, OUT_GATE, CELL = 0, 1, 2, 3
+FORGET_IN_TILES = (0, 1, 2, 3)
+OUT_TILES = (4, 5)
+CELL_TILES = (6, 7)
 
 COL_B, COL_G_IH, COL_B_IH, COL_G_HH, COL_B_HH = 0, 8, 16, 24, 32
 COL_G_C, COL_B_C = 40, 42
@@ -37,7 +39,7 @@ VECTOR_COLS = 44
 FLOPS = 2 * BATCH * IN * GATES + 2 * BATCH * HID * GATES
 
 
-def batch_norm_scale(nc, pool, neg_half, sources, gamma, label):
+def centre_and_rstd(nc, pool, neg_half, sources, gains, centred, label):
     count = len(sources)
     stats = pool.tile([P, count, 6], F32, name=label + "_stats")
     mean_var = pool.tile([P, count, 2], F32, name=label + "_mean_var")
@@ -49,13 +51,16 @@ def batch_norm_scale(nc, pool, neg_half, sources, gamma, label):
     nc.vector.tensor_scalar_add(out=var_eps[:], in0=mean_var[:, :, 1], scalar1=EPS)
     rstd = pool.tile([P, count], F32, name=label + "_rstd")
     nc.gpsimd.tensor_tensor(out=rstd[:], in0=var_eps[:], in1=neg_half[:, 0:count], op=ALU.pow)
-    scale = pool.tile([P, count], F32, name=label + "_scale")
-    nc.vector.tensor_mul(out=scale[:], in0=rstd[:], in1=gamma)
-    shift = pool.tile([P, count], F32, name=label + "_shift")
-    nc.vector.scalar_tensor_tensor(
-        out=shift[:], in0=mean_var[:, :, 0], scalar=-1.0, in1=scale[:], op0=ALU.mult, op1=ALU.mult
-    )
-    return scale, shift
+    for t in range(count):
+        nc.vector.tensor_scalar(
+            out=centred[t],
+            in0=sources[t],
+            scalar1=mean_var[:, t, 0:1],
+            scalar2=gains[t],
+            op0=ALU.subtract,
+            op1=ALU.mult,
+        )
+    return rstd
 
 
 def tile_lstmcell_k_kernel(
@@ -64,9 +69,9 @@ def tile_lstmcell_k_kernel(
     nc = tc.nc
     with ExitStack() as whole:
         keep = whole.enter_context(tc.tile_pool(name="keep", bufs=1))
-        w_pool = whole.enter_context(tc.tile_pool(name="w_words", bufs=PASSES))
+        w_pool = whole.enter_context(tc.tile_pool(name="w_words", bufs=BLOCKS))
 
-        w_planes = keep.tile([P, PASSES // PLANES_PER_TILE, GATES], U8, align_bytes=64)
+        w_planes = keep.tile([P, BLOCKS, GATES], U8, align_bytes=64)
         nc.vector.memset(w_planes[:].bitcast(I32), 0)
         vector_rows = keep.tile([P, P], BF16)
         nc.vector.memset(vector_rows[:], 0.0)
@@ -83,17 +88,17 @@ def tile_lstmcell_k_kernel(
 
         with ExitStack() as head:
             stage = head.enter_context(tc.tile_pool(name="stage", bufs=1))
-            x_pool = head.enter_context(tc.tile_pool(name="x", bufs=X_CHUNKS))
+            x_pool = head.enter_context(tc.tile_pool(name="x", bufs=BLOCKS))
             grouped_pool = head.enter_context(tc.tile_pool(name="grouped", bufs=3))
 
             w_hh_rows = stage.tile([P, TILES, HID], BF16)
             nc.sync.dma_start(out=w_hh_rows[:], in_=w_hh.rearrange("(j p) k -> p j k", p=P))
-            x_chunks = []
-            chunk_cols = X_CHUNK_PASSES * K_PASS
-            for i in range(X_CHUNKS):
-                x_chunk = x_pool.tile([P, chunk_cols], BF16)
-                nc.sync.dma_start(out=x_chunk[:], in_=x[:, i * chunk_cols : (i + 1) * chunk_cols])
-                x_chunks.append(x_chunk)
+            x_blocks = []
+            block_cols = BLOCK_PASSES * K_PASS
+            for m in range(BLOCKS):
+                x_block = x_pool.tile([P, block_cols], BF16)
+                nc.sync.dma_start(out=x_block[:], in_=x[:, m * block_cols : (m + 1) * block_cols])
+                x_blocks.append(x_block)
 
             h_rows = stage.tile([P, HID], BF16)
             nc.scalar.dma_start(out=h_rows[:], in_=h[:, :])
@@ -113,23 +118,35 @@ def tile_lstmcell_k_kernel(
                     out=vector_rows[col : col + rows, :], in_=vector.rearrange("(r e) -> r e", e=P)
                 )
 
-            for m in range(PASSES // PLANES_PER_TILE):
-                for quad in range(4):
-                    nc.sync.dma_start(
-                        out=w_planes[32 * quad : 32 * quad + 16, m, :].bitcast(I32),
-                        in_=w_ih_scales[
-                            PLANES_PER_TILE * m : PLANES_PER_TILE * (m + 1), 4 * quad : 4 * quad + 4, :
-                        ].bitcast(I32),
+            scale_rows = w_ih_scales.rearrange("(m s) (quad r) n -> s r quad m n", s=BLOCK_PASSES, r=4)
+            for s in range(BLOCK_PASSES):
+                for r in range(4):
+                    nc.gpsimd.dma_start(
+                        out=w_planes[4 * s + r : P : 32, :, :].bitcast(F32),
+                        in_=scale_rows[s, r].bitcast(F32),
                     )
 
-            w_words = []
-            for g in range(PASSES):
-                words = w_pool.tile([P, GATES], U32, align_bytes=64)
+            w_blocks = [
+                w_pool.tile([P, BLOCK_PASSES, GATES], U32, align_bytes=64, name="w_block", tag="w")
+                for m in range(BLOCKS)
+            ]
+
+            def load_w(m, first_tile, tile_count):
+                cols = slice(first_tile * P, (first_tile + tile_count) * P)
                 nc.sync.dma_start(
-                    out=words[:].bitcast(I32),
-                    in_=w_ih_words[g].rearrange("p n t -> p (n t)").bitcast(I32),
+                    out=w_blocks[m][:, :, cols].bitcast(I32),
+                    in_=w_ih_words[BLOCK_PASSES * m : BLOCK_PASSES * (m + 1), :, cols, :]
+                    .rearrange("g p n t -> p g (n t)")
+                    .bitcast(I32),
                 )
-                w_words.append(words)
+
+            for m in range(EARLY_BLOCKS):
+                load_w(m, 0, TILES)
+            for m in range(EARLY_BLOCKS, BLOCKS):
+                load_w(m, FORGET_IN_TILES[0], len(FORGET_IN_TILES))
+                load_w(m, CELL_TILES[0], len(CELL_TILES))
+            for m in range(EARLY_BLOCKS, BLOCKS):
+                load_w(m, OUT_TILES[0], len(OUT_TILES))
 
             head_psum = head.enter_context(tc.psum_pool(name="head_psum", bufs=1))
             hh_psum = head.enter_context(tc.psum_pool(name="hh_psum", bufs=2))
@@ -160,8 +177,8 @@ def tile_lstmcell_k_kernel(
                 nc.scalar.copy(
                     out=w_hh_t[:, s, :].rearrange("p (j n) -> p j n", j=TILES), in_=w_hh_bank[:]
                 )
+            hh_part = keep.tile([P, TILES, BATCH], F32)
             tiles_per_bank = 4
-            hh_tiles = []
             for bank in range(TILES // tiles_per_bank):
                 hh_bank = hh_psum.tile([P, tiles_per_bank, BATCH], F32, tag="hh")
                 for t in range(tiles_per_bank):
@@ -174,144 +191,167 @@ def tile_lstmcell_k_kernel(
                             start=(s == 0),
                             stop=(s == HALVES - 1),
                         )
-                    hh_tiles.append(hh_bank[:, t, :])
-            hh_scale, hh_shift = batch_norm_scale(
-                nc, stage, neg_half, hh_tiles, vectors[:, COL_G_HH : COL_G_HH + TILES], "hh"
+                bank_tiles = slice(bank * tiles_per_bank, (bank + 1) * tiles_per_bank)
+                nc.scalar.copy(out=hh_part[:, bank_tiles, :], in_=hh_bank[:])
+            bias_sum = stage.tile([P, TILES], F32)
+            nc.vector.tensor_add(
+                out=bias_sum[:],
+                in0=vectors[:, COL_B : COL_B + TILES],
+                in1=vectors[:, COL_B_IH : COL_B_IH + TILES],
             )
-            for col in (COL_B, COL_B_IH, COL_B_HH):
-                nc.vector.tensor_add(out=hh_shift[:], in0=hh_shift[:], in1=vectors[:, col : col + TILES])
-            hh_part = keep.tile([P, TILES, BATCH], F32)
+            nc.vector.tensor_add(
+                out=bias_sum[:], in0=bias_sum[:], in1=vectors[:, COL_B_HH : COL_B_HH + TILES]
+            )
+            hh_tiles = [hh_part[:, j, :] for j in range(TILES)]
+            hh_rstd = centre_and_rstd(
+                nc,
+                stage,
+                neg_half,
+                hh_tiles,
+                [vectors[:, COL_G_HH + j : COL_G_HH + j + 1] for j in range(TILES)],
+                hh_tiles,
+                "hh",
+            )
             for j in range(TILES):
                 nc.scalar.activation(
                     out=hh_part[:, j, :],
-                    in_=hh_tiles[j],
+                    in_=hh_part[:, j, :],
                     func=ACT.Identity,
-                    scale=hh_scale[:, j : j + 1],
-                    bias=hh_shift[:, j : j + 1],
+                    scale=hh_rstd[:, j : j + 1],
+                    bias=bias_sum[:, j : j + 1],
                 )
 
             x_words = keep.tile([P, PASSES, BATCH], U32, align_bytes=64)
             x_planes = keep.tile([P, PASSES, BATCH], U8, align_bytes=64)
             passes_per_bank = 2
-            for i in range(X_CHUNKS):
-                pairs = x_chunks[i][:].bitcast(F32)
-                grouped = grouped_pool.tile([P, X_CHUNK_PASSES, BATCH, 4], BF16, align_bytes=64)
-                for first in range(0, X_CHUNK_PASSES, passes_per_bank):
+            for m in range(BLOCKS):
+                pairs = x_blocks[m][:].bitcast(F32)
+                grouped = grouped_pool.tile([P, BLOCK_PASSES, BATCH, 4], BF16, align_bytes=64)
+                for first in range(0, BLOCK_PASSES, passes_per_bank):
                     x_bank = x_psum.tile([P, passes_per_bank, 2, BATCH], F32)
                     for r in range(passes_per_bank):
-                        start_word = (first + r) * (K_PASS // 2)
+                        first_word = (first + r) * (K_PASS // 2)
                         for u in range(2):
                             nc.tensor.transpose(
                                 x_bank[:, r, u, :],
-                                pairs[:, start_word + u : start_word + K_PASS // 2 : 2],
+                                pairs[:, first_word + u : first_word + K_PASS // 2 : 2],
                                 ident_f32[:],
                             )
                     nc.scalar.copy(
                         out=grouped[:].bitcast(F32)[:, first : first + passes_per_bank, :, :],
                         in_=x_bank[:].rearrange("p r u b -> p r b u"),
                     )
-                chunk = slice(i * X_CHUNK_PASSES, (i + 1) * X_CHUNK_PASSES)
+                block = slice(m * BLOCK_PASSES, (m + 1) * BLOCK_PASSES)
                 nc.vector.quantize_mx(
-                    out=x_words[:, chunk, :].rearrange("p g b -> p (g b)").bitcast(FP8X4),
-                    scales=x_planes[:, chunk, :].rearrange("p g b -> p (g b)"),
+                    out=x_words[:, block, :].rearrange("p g b -> p (g b)").bitcast(FP8X4),
+                    scales=x_planes[:, block, :].rearrange("p g b -> p (g b)"),
                     in_=grouped[:].rearrange("p g b t -> p (g b t)"),
                 )
 
         acc_pool = whole.enter_context(tc.psum_pool(name="acc", bufs=1))
         tail = whole.enter_context(tc.tile_pool(name="tail", bufs=1))
         acc = [acc_pool.tile([P, BATCH], F32, name="acc%d" % j) for j in range(TILES)]
-        for g in range(PASSES):
-            first_row = 4 * (g % PLANES_PER_TILE)
-            for j in range(TILES):
-                cols = slice(j * P, (j + 1) * P)
-                nc.tensor.matmul_mx(
-                    out=acc[j][:],
-                    lhsT=w_words[g][:, cols].bitcast(FP8X4),
-                    lhsT_scale=w_planes[first_row:P, g // PLANES_PER_TILE, cols],
-                    rhs=x_words[:, g, :].bitcast(FP8X4),
-                    rhs_scale=x_planes[:, g, :],
-                    start=(g == 0),
-                    stop=(g == PASSES - 1),
-                )
 
-        gate_sum = tail.tile([P, TILES, BATCH], F32)
+        def mx_passes(first_pass, last_pass, tiles):
+            for g in range(first_pass, last_pass):
+                m, s = divmod(g, BLOCK_PASSES)
+                for j in tiles:
+                    cols = slice(j * P, (j + 1) * P)
+                    nc.tensor.matmul_mx(
+                        out=acc[j][:],
+                        lhsT=w_blocks[m][:, s, cols].bitcast(FP8X4),
+                        lhsT_scale=w_planes[4 * s : P, m, cols],
+                        rhs=x_words[:, g, :].bitcast(FP8X4),
+                        rhs_scale=x_planes[:, g, :],
+                        start=(g == 0),
+                        stop=(g == PASSES - 1),
+                    )
+
         gate = tail.tile([P, TILES, BATCH], F32)
 
-        def finish_gates(first_gate, gate_count, label):
-            tiles = range(first_gate * HALVES, (first_gate + gate_count) * HALVES)
-            scale, shift = batch_norm_scale(
+        def finish_gates(tiles, func, label):
+            rstd = centre_and_rstd(
                 nc,
                 tail,
                 neg_half,
                 [acc[j][:] for j in tiles],
-                vectors[:, COL_G_IH + tiles[0] : COL_G_IH + tiles[0] + len(tiles)],
+                [vectors[:, COL_G_IH + j : COL_G_IH + j + 1] for j in tiles],
+                [gate[:, j, :] for j in tiles],
                 label,
             )
             for t, j in enumerate(tiles):
                 nc.vector.scalar_tensor_tensor(
-                    out=gate_sum[:, j, :],
-                    in0=acc[j][:],
-                    scalar=scale[:, t : t + 1],
+                    out=gate[:, j, :],
+                    in0=gate[:, j, :],
+                    scalar=rstd[:, t : t + 1],
                     in1=hh_part[:, j, :],
                     op0=ALU.mult,
                     op1=ALU.add,
                 )
-                nc.scalar.activation(
-                    out=gate[:, j, :],
-                    in_=gate_sum[:, j, :],
-                    func=ACT.Tanh if j // HALVES == CELL else ACT.Sigmoid,
-                    bias=shift[:, t : t + 1],
-                )
+                nc.scalar.activation(out=gate[:, j, :], in_=gate[:, j, :], func=func)
 
-        def gate_tiles(which):
-            return gate[:, which * HALVES : (which + 1) * HALVES, :]
+        def to_rows(result_t, bank_tag):
+            bank = acc_pool.tile([P, HALVES, P], F32, tag=bank_tag, name="rows_" + bank_tag)
+            for s in range(HALVES):
+                nc.tensor.transpose(bank[:, s, :], result_t[:, s, :], ident_f32[:])
+            return bank[:].rearrange("p s n -> p (s n)")
 
-        finish_gates(FORGET, 2, "forget_in")
-        finish_gates(CELL, 1, "cell")
-        finish_gates(OUT_GATE, 1, "out")
+        first_late = EARLY_BLOCKS * BLOCK_PASSES
+        mx_passes(0, first_late, range(TILES))
+        mx_passes(first_late, PASSES, FORGET_IN_TILES + CELL_TILES)
+        mx_passes(first_late, PASSES, OUT_TILES)
 
+        finish_gates(FORGET_IN_TILES, ACT.Sigmoid, "forget_in")
+        finish_gates(CELL_TILES, ACT.Tanh, "cell")
         kept = tail.tile([P, HALVES, BATCH], F32)
-        nc.vector.tensor_mul(out=kept[:], in0=gate_tiles(FORGET), in1=c_t[:])
+        nc.vector.tensor_mul(out=kept[:], in0=gate[:, 0:HALVES, :], in1=c_t[:])
         added = tail.tile([P, HALVES, BATCH], F32)
-        nc.vector.tensor_mul(out=added[:], in0=gate_tiles(IN_GATE), in1=gate_tiles(CELL))
+        nc.vector.tensor_mul(
+            out=added[:],
+            in0=gate[:, HALVES : 2 * HALVES, :],
+            in1=gate[:, CELL_TILES[0] : CELL_TILES[0] + HALVES, :],
+        )
         c_raw = tail.tile([P, HALVES, BATCH], F32)
         nc.vector.tensor_add(out=c_raw[:], in0=kept[:], in1=added[:])
-        c_scale, c_shift = batch_norm_scale(
+        c_centred = tail.tile([P, HALVES, BATCH], F32)
+        c_rstd = centre_and_rstd(
             nc,
             tail,
             neg_half,
             [c_raw[:, s, :] for s in range(HALVES)],
-            vectors[:, COL_G_C : COL_G_C + HALVES],
+            [vectors[:, COL_G_C + s : COL_G_C + s + 1] for s in range(HALVES)],
+            [c_centred[:, s, :] for s in range(HALVES)],
             "c",
         )
-        nc.vector.tensor_add(
-            out=c_shift[:], in0=c_shift[:], in1=vectors[:, COL_B_C : COL_B_C + HALVES]
-        )
         c_next_t = tail.tile([P, HALVES, BATCH], F32)
-        tanh_c = tail.tile([P, HALVES, BATCH], F32)
+        tanh_c_t = tail.tile([P, HALVES, BATCH], F32)
         for s in range(HALVES):
+            nc.scalar.activation(
+                out=tanh_c_t[:, s, :],
+                in_=c_centred[:, s, :],
+                func=ACT.Tanh,
+                scale=c_rstd[:, s : s + 1],
+                bias=vectors[:, COL_B_C + s : COL_B_C + s + 1],
+            )
             nc.vector.tensor_scalar(
                 out=c_next_t[:, s, :],
-                in0=c_raw[:, s, :],
-                scalar1=c_scale[:, s : s + 1],
-                scalar2=c_shift[:, s : s + 1],
+                in0=c_centred[:, s, :],
+                scalar1=c_rstd[:, s : s + 1],
+                scalar2=vectors[:, COL_B_C + s : COL_B_C + s + 1],
                 op0=ALU.mult,
                 op1=ALU.add,
             )
-            nc.scalar.activation(
-                out=tanh_c[:, s, :],
-                in_=c_raw[:, s, :],
-                func=ACT.Tanh,
-                scale=c_scale[:, s : s + 1],
-                bias=c_shift[:, s : s + 1],
-            )
-        h_next_t = tail.tile([P, HALVES, BATCH], F32)
-        nc.vector.tensor_mul(out=h_next_t[:], in0=gate_tiles(OUT_GATE), in1=tanh_c[:])
+        tanh_c = tail.tile([P, HID], F32)
+        nc.scalar.copy(out=tanh_c[:], in_=to_rows(tanh_c_t, "acc0"))
+        c_next = tail.tile([P, HID], F32)
+        nc.scalar.copy(out=c_next[:], in_=to_rows(c_next_t, "acc1"))
+        nc.sync.dma_start(out=out_0[:, :], in_=c_next[:])
 
-        for result_t, out, bank_tag in ((c_next_t, out_0, "acc0"), (h_next_t, out_1, "acc1")):
-            result_bank = acc_pool.tile([P, HALVES, P], F32, tag=bank_tag, name="t_" + bank_tag)
-            for s in range(HALVES):
-                nc.tensor.transpose(result_bank[:, s, :], result_t[:, s, :], ident_f32[:])
-            result = tail.tile([P, HID], F32, name="r_" + bank_tag)
-            nc.scalar.copy(out=result[:].rearrange("p (s n) -> p s n", s=HALVES), in_=result_bank[:])
-            nc.sync.dma_start(out=out[:, :], in_=result[:])
+        finish_gates(OUT_TILES, ACT.Sigmoid, "out")
+        h_next = tail.tile([P, HID], F32)
+        nc.vector.tensor_mul(
+            out=h_next[:],
+            in0=to_rows(gate[:, OUT_TILES[0] : OUT_TILES[0] + HALVES, :], "acc2"),
+            in1=tanh_c[:],
+        )
+        nc.sync.dma_start(out=out_1[:, :], in_=h_next[:])

@@ -25,6 +25,7 @@ BLOCK_PASSES = 4
 BLOCKS = PASSES // BLOCK_PASSES
 LATE_BLOCKS = 6
 EARLY_BLOCKS = BLOCKS - LATE_BLOCKS
+FIRST_SCALE_BLOCKS = 2
 
 TILES = GATES // P
 HALVES = HID // P
@@ -72,7 +73,8 @@ def tile_lstmcell_k_kernel(
         w_pool = whole.enter_context(tc.tile_pool(name="w_words", bufs=BLOCKS))
 
         w_planes = keep.tile([P, BLOCKS, GATES], U8, align_bytes=64)
-        nc.vector.memset(w_planes[:].bitcast(I32), 0)
+        for m in range(BLOCKS):
+            nc.vector.memset(w_planes[:, m, :].bitcast(I32), 0)
         vector_rows = keep.tile([P, P], BF16)
         nc.vector.memset(vector_rows[:], 0.0)
         neg_half = keep.tile([P, TILES], F32)
@@ -118,13 +120,17 @@ def tile_lstmcell_k_kernel(
                     out=vector_rows[col : col + rows, :], in_=vector.rearrange("(r e) -> r e", e=P)
                 )
 
-            scale_rows = w_ih_scales.rearrange("(m s) (quad r) n -> s r quad m n", s=BLOCK_PASSES, r=4)
-            for s in range(BLOCK_PASSES):
-                for r in range(4):
+            def load_scales(m):
+                for quad in range(4):
                     nc.gpsimd.dma_start(
-                        out=w_planes[4 * s + r : P : 32, :, :].bitcast(F32),
-                        in_=scale_rows[s, r].bitcast(F32),
+                        out=w_planes[32 * quad : 32 * quad + 16, m, :].bitcast(F32),
+                        in_=w_ih_scales[
+                            BLOCK_PASSES * m : BLOCK_PASSES * (m + 1), 4 * quad : 4 * quad + 4, :
+                        ].bitcast(F32),
                     )
+
+            for m in range(FIRST_SCALE_BLOCKS):
+                load_scales(m)
 
             w_blocks = [
                 w_pool.tile([P, BLOCK_PASSES, GATES], U32, align_bytes=64, name="w_block", tag="w")
@@ -220,6 +226,9 @@ def tile_lstmcell_k_kernel(
                     scale=hh_rstd[:, j : j + 1],
                     bias=bias_sum[:, j : j + 1],
                 )
+
+            for m in range(FIRST_SCALE_BLOCKS, BLOCKS):
+                load_scales(m)
 
             x_words = keep.tile([P, PASSES, BATCH], U32, align_bytes=64)
             x_planes = keep.tile([P, PASSES, BATCH], U8, align_bytes=64)

@@ -148,11 +148,9 @@ def tile_lstmcell_k_kernel(
 
             for m in range(EARLY_BLOCKS):
                 load_w(m, 0, TILES)
-            for m in range(EARLY_BLOCKS, BLOCKS):
-                load_w(m, FORGET_IN_TILES[0], len(FORGET_IN_TILES))
-                load_w(m, CELL_TILES[0], len(CELL_TILES))
-            for m in range(EARLY_BLOCKS, BLOCKS):
-                load_w(m, OUT_TILES[0], len(OUT_TILES))
+            for late_tiles in (FORGET_IN_TILES, CELL_TILES, OUT_TILES):
+                for m in range(EARLY_BLOCKS, BLOCKS):
+                    load_w(m, late_tiles[0], len(late_tiles))
 
             head_psum = head.enter_context(tc.psum_pool(name="head_psum", bufs=1))
             hh_psum = head.enter_context(tc.psum_pool(name="hh_psum", bufs=2))
@@ -307,8 +305,8 @@ def tile_lstmcell_k_kernel(
 
         first_late = EARLY_BLOCKS * BLOCK_PASSES
         mx_passes(0, first_late, range(TILES))
-        mx_passes(first_late, PASSES, FORGET_IN_TILES + CELL_TILES)
-        mx_passes(first_late, PASSES, OUT_TILES)
+        for late_tiles in (FORGET_IN_TILES, CELL_TILES, OUT_TILES):
+            mx_passes(first_late, PASSES, late_tiles)
 
         finish_gates(FORGET_IN_TILES, ACT.Sigmoid, "forget_in")
         finish_gates(CELL_TILES, ACT.Tanh, "cell")

@@ -255,6 +255,7 @@ def tile_lstmcell_k_kernel(
                     in_=grouped[:].rearrange("p g b t -> p (g b t)"),
                 )
 
+        whole.enter_context(tc.manual_schedule(engines={mybir.EngineType.PE}))
         acc_pool = whole.enter_context(tc.psum_pool(name="acc", bufs=1))
         tail = whole.enter_context(tc.tile_pool(name="tail", bufs=1))
         acc = [acc_pool.tile([P, BATCH], F32, name="acc%d" % j) for j in range(TILES)]

@@ -255,7 +255,7 @@ def tile_lstmcell_k_kernel(
                     in_=grouped[:].rearrange("p g b t -> p (g b t)"),
                 )
 
-        whole.enter_context(tc.manual_schedule(engines={mybir.EngineType.PE}))
+        whole.enter_context(tc.manual_schedule())
         acc_pool = whole.enter_context(tc.psum_pool(name="acc", bufs=1))
         tail = whole.enter_context(tc.tile_pool(name="tail", bufs=1))
         acc = [acc_pool.tile([P, BATCH], F32, name="acc%d" % j) for j in range(TILES)]
@@ -310,9 +310,9 @@ def tile_lstmcell_k_kernel(
             mx_passes(first_late, PASSES, late_tiles)
 
         finish_gates(FORGET_IN_TILES, ACT.Sigmoid, "forget_in")
-        finish_gates(CELL_TILES, ACT.Tanh, "cell")
         kept = tail.tile([P, HALVES, BATCH], F32)
         nc.vector.tensor_mul(out=kept[:], in0=gate[:, 0:HALVES, :], in1=c_t[:])
+        finish_gates(CELL_TILES, ACT.Tanh, "cell")
         added = tail.tile([P, HALVES, BATCH], F32)
         nc.vector.tensor_mul(
             out=added[:],

@@ -26,6 +26,8 @@ BLOCKS = PASSES // BLOCK_PASSES
 LATE_BLOCKS = 6
 EARLY_BLOCKS = BLOCKS - LATE_BLOCKS
 FIRST_SCALE_BLOCKS = 2
+FIRST_LOAD_PASSES = (1, 2)
+VECTOR_SHARE = 3
 
 TILES = GATES // P
 HALVES = HID // P
@@ -137,20 +139,23 @@ def tile_lstmcell_k_kernel(
                 for m in range(BLOCKS)
             ]
 
-            def load_w(m, first_tile, tile_count):
-                cols = slice(first_tile * P, (first_tile + tile_count) * P)
+            def load_w(m, tiles, first_place=0, last_place=BLOCK_PASSES):
+                cols = slice(tiles[0] * P, (tiles[-1] + 1) * P)
+                first_pass = BLOCK_PASSES * m
                 nc.sync.dma_start(
-                    out=w_blocks[m][:, :, cols].bitcast(I32),
-                    in_=w_ih_words[BLOCK_PASSES * m : BLOCK_PASSES * (m + 1), :, cols, :]
+                    out=w_blocks[m][:, first_place:last_place, cols].bitcast(I32),
+                    in_=w_ih_words[first_pass + first_place : first_pass + last_place, :, cols, :]
                     .rearrange("g p n t -> p g (n t)")
                     .bitcast(I32),
                 )
 
             for m in range(EARLY_BLOCKS):
-                load_w(m, 0, TILES)
+                load_passes = FIRST_LOAD_PASSES[m]
+                for first_place in range(0, BLOCK_PASSES, load_passes):
+                    load_w(m, range(TILES), first_place, first_place + load_passes)
             for late_tiles in (FORGET_IN_TILES, CELL_TILES, OUT_TILES):
                 for m in range(EARLY_BLOCKS, BLOCKS):
-                    load_w(m, late_tiles[0], len(late_tiles))
+                    load_w(m, late_tiles)
 
             head_psum = head.enter_context(tc.psum_pool(name="head_psum", bufs=1))
             hh_psum = head.enter_context(tc.psum_pool(name="hh_psum", bufs=2))
@@ -244,10 +249,13 @@ def tile_lstmcell_k_kernel(
                                 pairs[:, first_word + u : first_word + K_PASS // 2 : 2],
                                 ident_f32[:],
                             )
-                    nc.scalar.copy(
-                        out=grouped[:].bitcast(F32)[:, first : first + passes_per_bank, :, :],
-                        in_=x_bank[:].rearrange("p r u b -> p r b u"),
-                    )
+                    bank_index = (m * BLOCK_PASSES + first) // passes_per_bank
+                    words_out = grouped[:].bitcast(F32)[:, first : first + passes_per_bank, :, :]
+                    words_in = x_bank[:].rearrange("p r u b -> p r b u")
+                    if bank_index % VECTOR_SHARE == VECTOR_SHARE - 1:
+                        nc.vector.tensor_copy(out=words_out, in_=words_in)
+                    else:
+                        nc.scalar.copy(out=words_out, in_=words_in)
                 block = slice(m * BLOCK_PASSES, (m + 1) * BLOCK_PASSES)
                 nc.vector.quantize_mx(
                     out=x_words[:, block, :].rearrange("p g b -> p (g b)").bitcast(FP8X4),

@@ -25,7 +25,6 @@ BLOCK_PASSES = 4
 BLOCKS = PASSES // BLOCK_PASSES
 LATE_BLOCKS = 6
 EARLY_BLOCKS = BLOCKS - LATE_BLOCKS
-FIRST_SCALE_BLOCKS = 2
 FIRST_LOAD_PASSES = (1, 2)
 VECTOR_SHARE = 3
 
@@ -131,7 +130,7 @@ def tile_lstmcell_k_kernel(
                         ].bitcast(F32),
                     )
 
-            for m in range(FIRST_SCALE_BLOCKS):
+            for m in range(BLOCKS):
                 load_scales(m)
 
             w_blocks = [
@@ -229,9 +228,6 @@ def tile_lstmcell_k_kernel(
                     scale=hh_rstd[:, j : j + 1],
                     bias=bias_sum[:, j : j + 1],
                 )
-
-            for m in range(FIRST_SCALE_BLOCKS, BLOCKS):
-                load_scales(m)
 
             x_words = keep.tile([P, PASSES, BATCH], U32, align_bytes=64)
             x_planes = keep.tile([P, PASSES, BATCH], U8, align_bytes=64)

@@ -18,6 +18,8 @@ IN = 16384
 HID = 256
 GATES = 4 * HID
 EPS = 1e-5
+TRIPLE = 3
+STATS = 2 * TRIPLE
 
 K_PASS = 512
 PASSES = IN // K_PASS
@@ -41,18 +43,15 @@ VECTOR_COLS = 44
 FLOPS = 2 * BATCH * IN * GATES + 2 * BATCH * HID * GATES
 
 
-def centre_and_rstd(nc, pool, neg_half, sources, gains, centred, label):
+def centre_and_rstd(nc, pool, neg_half, stats, sources, gains, centred, label):
     count = len(sources)
-    stats = pool.tile([P, count, 6], F32, name=label + "_stats")
     mean_var = pool.tile([P, count, 2], F32, name=label + "_mean_var")
     for t in range(count):
-        nc.vector.bn_stats(out=stats[:, t, :], in_=sources[t])
+        nc.vector.bn_stats(out=stats[:, t, 0:STATS], in_=sources[t])
     for t in range(count):
         nc.vector.bn_aggr(out=mean_var[:, t, :], in_=stats[:, t, :])
-    var_eps = pool.tile([P, count], F32, name=label + "_var_eps")
-    nc.vector.tensor_scalar_add(out=var_eps[:], in0=mean_var[:, :, 1], scalar1=EPS)
     rstd = pool.tile([P, count], F32, name=label + "_rstd")
-    nc.gpsimd.tensor_tensor(out=rstd[:], in0=var_eps[:], in1=neg_half[:, 0:count], op=ALU.pow)
+    nc.gpsimd.tensor_tensor(out=rstd[:], in0=mean_var[:, :, 1], in1=neg_half[:, 0:count], op=ALU.pow)
     for t in range(count):
         nc.vector.tensor_scalar(
             out=centred[t],
@@ -80,6 +79,9 @@ def tile_lstmcell_k_kernel(
         nc.vector.memset(vector_rows[:], 0.0)
         neg_half = keep.tile([P, TILES], F32)
         nc.vector.memset(neg_half[:], -0.5)
+        stats = keep.tile([P, 2 * TILES + HALVES, STATS + TRIPLE], F32)
+        nc.vector.memset(stats[:, :, STATS:], 0.0)
+        nc.vector.memset(stats[:, :, STATS + TRIPLE - 1 :], BATCH * EPS)
         ident_f32 = keep.tile([P, P], F32)
         make_identity(nc, ident_f32[:])
         ident_bf16 = keep.tile([P, P], BF16)
@@ -215,6 +217,7 @@ def tile_lstmcell_k_kernel(
                 nc,
                 stage,
                 neg_half,
+                stats[:, 0:TILES, :],
                 hh_tiles,
                 [vectors[:, COL_G_HH + j : COL_G_HH + j + 1] for j in range(TILES)],
                 hh_tiles,
@@ -264,20 +267,26 @@ def tile_lstmcell_k_kernel(
         tail = whole.enter_context(tc.tile_pool(name="tail", bufs=1))
         acc = [acc_pool.tile([P, BATCH], F32, name="acc%d" % j) for j in range(TILES)]
 
-        def mx_passes(first_pass, last_pass, tiles):
-            for g in range(first_pass, last_pass):
-                m, s = divmod(g, BLOCK_PASSES)
+        def mx_pass(g, j):
+            m, s = divmod(g, BLOCK_PASSES)
+            cols = slice(j * P, (j + 1) * P)
+            nc.tensor.matmul_mx(
+                out=acc[j][:],
+                lhsT=w_blocks[m][:, s, cols].bitcast(FP8X4),
+                lhsT_scale=w_planes[4 * s : P, m, cols],
+                rhs=x_words[:, g, :].bitcast(FP8X4),
+                rhs_scale=x_planes[:, g, :],
+                start=(g == 0),
+                stop=(g == PASSES - 1),
+            )
+
+        def late_passes(tiles):
+            for g in range(EARLY_BLOCKS * BLOCK_PASSES, PASSES - BLOCK_PASSES):
                 for j in tiles:
-                    cols = slice(j * P, (j + 1) * P)
-                    nc.tensor.matmul_mx(
-                        out=acc[j][:],
-                        lhsT=w_blocks[m][:, s, cols].bitcast(FP8X4),
-                        lhsT_scale=w_planes[4 * s : P, m, cols],
-                        rhs=x_words[:, g, :].bitcast(FP8X4),
-                        rhs_scale=x_planes[:, g, :],
-                        start=(g == 0),
-                        stop=(g == PASSES - 1),
-                    )
+                    mx_pass(g, j)
+            for j in tiles:
+                for g in range(PASSES - BLOCK_PASSES, PASSES):
+                    mx_pass(g, j)
 
         gate = tail.tile([P, TILES, BATCH], F32)
 
@@ -286,6 +295,7 @@ def tile_lstmcell_k_kernel(
                 nc,
                 tail,
                 neg_half,
+                stats[:, TILES + tiles[0] : TILES + tiles[-1] + 1, :],
                 [acc[j][:] for j in tiles],
                 [vectors[:, COL_G_IH + j : COL_G_IH + j + 1] for j in tiles],
                 [gate[:, j, :] for j in tiles],
@@ -308,28 +318,32 @@ def tile_lstmcell_k_kernel(
                 nc.tensor.transpose(bank[:, s, :], result_t[:, s, :], ident_f32[:])
             return bank[:].rearrange("p s n -> p (s n)")
 
-        first_late = EARLY_BLOCKS * BLOCK_PASSES
-        mx_passes(0, first_late, range(TILES))
+        for g in range(EARLY_BLOCKS * BLOCK_PASSES):
+            for j in range(TILES):
+                mx_pass(g, j)
         for late_tiles in (FORGET_IN_TILES, CELL_TILES, OUT_TILES):
-            mx_passes(first_late, PASSES, late_tiles)
+            late_passes(late_tiles)
 
         finish_gates(FORGET_IN_TILES, ACT.Sigmoid, "forget_in")
         kept = tail.tile([P, HALVES, BATCH], F32)
         nc.vector.tensor_mul(out=kept[:], in0=gate[:, 0:HALVES, :], in1=c_t[:])
         finish_gates(CELL_TILES, ACT.Tanh, "cell")
         added = tail.tile([P, HALVES, BATCH], F32)
-        nc.vector.tensor_mul(
-            out=added[:],
-            in0=gate[:, HALVES : 2 * HALVES, :],
-            in1=gate[:, CELL_TILES[0] : CELL_TILES[0] + HALVES, :],
-        )
+        for s in range(HALVES):
+            nc.vector.tensor_mul(
+                out=added[:, s, :],
+                in0=gate[:, HALVES + s, :],
+                in1=gate[:, CELL_TILES[s], :],
+            )
         c_raw = tail.tile([P, HALVES, BATCH], F32)
-        nc.vector.tensor_add(out=c_raw[:], in0=kept[:], in1=added[:])
+        for s in range(HALVES):
+            nc.vector.tensor_add(out=c_raw[:, s, :], in0=kept[:, s, :], in1=added[:, s, :])
         c_centred = tail.tile([P, HALVES, BATCH], F32)
         c_rstd = centre_and_rstd(
             nc,
             tail,
             neg_half,
+            stats[:, 2 * TILES : 2 * TILES + HALVES, :],
             [c_raw[:, s, :] for s in range(HALVES)],
             [vectors[:, COL_G_C + s : COL_G_C + s + 1] for s in range(HALVES)],
             [c_centred[:, s, :] for s in range(HALVES)],
@@ -361,9 +375,9 @@ def tile_lstmcell_k_kernel(
 
         finish_gates(OUT_TILES, ACT.Sigmoid, "out")
         h_next = tail.tile([P, HID], F32)
-        nc.vector.tensor_mul(
-            out=h_next[:],
-            in0=to_rows(gate[:, OUT_TILES[0] : OUT_TILES[0] + HALVES, :], "acc2"),
-            in1=tanh_c[:],
-        )
+        for s, bank_tag in enumerate(("acc2", "acc3")):
+            bank = acc_pool.tile([P, P], F32, tag=bank_tag, name="rows_" + bank_tag)
+            nc.tensor.transpose(bank[:], gate[:, OUT_TILES[s], :], ident_f32[:])
+            cols = slice(s * P, (s + 1) * P)
+            nc.vector.tensor_mul(out=h_next[:, cols], in0=bank[:], in1=tanh_c[:, cols])
         nc.sync.dma_start(out=out_1[:, :], in_=h_next[:])

@@ -20,6 +20,7 @@ GATES = 4 * HID
 EPS = 1e-5
 TRIPLE = 3
 STATS = 2 * TRIPLE
+STATS_ROOM = 192
 
 K_PASS = 512
 PASSES = IN // K_PASS
@@ -79,7 +80,11 @@ def tile_lstmcell_k_kernel(
         nc.vector.memset(vector_rows[:], 0.0)
         neg_half = keep.tile([P, TILES], F32)
         nc.vector.memset(neg_half[:], -0.5)
-        stats = keep.tile([P, 2 * TILES + HALVES, STATS + TRIPLE], F32)
+        stats_count = 2 * TILES + HALVES
+        stats_room = keep.tile([P, STATS_ROOM], F32)
+        stats = stats_room[:, 0 : stats_count * (STATS + TRIPLE)].rearrange(
+            "p (t v) -> p t v", t=stats_count
+        )
         nc.vector.memset(stats[:, :, STATS:], 0.0)
         nc.vector.memset(stats[:, :, STATS + TRIPLE - 1 :], BATCH * EPS)
         ident_f32 = keep.tile([P, P], F32)

@@ -20,7 +20,6 @@ GATES = 4 * HID
 EPS = 1e-5
 TRIPLE = 3
 STATS = 2 * TRIPLE
-STATS_ROOM = 192
 
 K_PASS = 512
 PASSES = IN // K_PASS
@@ -30,6 +29,8 @@ LATE_BLOCKS = 6
 EARLY_BLOCKS = BLOCKS - LATE_BLOCKS
 FIRST_LOAD_PASSES = (1, 2)
 VECTOR_SHARE = 3
+
+DMA_ALIGN = 256
 
 TILES = GATES // P
 HALVES = HID // P
@@ -73,18 +74,14 @@ def tile_lstmcell_k_kernel(
         keep = whole.enter_context(tc.tile_pool(name="keep", bufs=1))
         w_pool = whole.enter_context(tc.tile_pool(name="w_words", bufs=BLOCKS))
 
-        w_planes = keep.tile([P, BLOCKS, GATES], U8, align_bytes=64)
+        w_planes = keep.tile([P, BLOCKS, GATES], U8, align_bytes=DMA_ALIGN)
         for m in range(BLOCKS):
             nc.vector.memset(w_planes[:, m, :].bitcast(I32), 0)
-        vector_rows = keep.tile([P, P], BF16)
+        vector_rows = keep.tile([P, P], BF16, align_bytes=DMA_ALIGN)
         nc.vector.memset(vector_rows[:], 0.0)
         neg_half = keep.tile([P, TILES], F32)
         nc.vector.memset(neg_half[:], -0.5)
-        stats_count = 2 * TILES + HALVES
-        stats_room = keep.tile([P, STATS_ROOM], F32)
-        stats = stats_room[:, 0 : stats_count * (STATS + TRIPLE)].rearrange(
-            "p (t v) -> p t v", t=stats_count
-        )
+        stats = keep.tile([P, 2 * TILES + HALVES, STATS + TRIPLE], F32)
         nc.vector.memset(stats[:, :, STATS:], 0.0)
         nc.vector.memset(stats[:, :, STATS + TRIPLE - 1 :], BATCH * EPS)
         ident_f32 = keep.tile([P, P], F32)
@@ -101,18 +98,18 @@ def tile_lstmcell_k_kernel(
             x_pool = head.enter_context(tc.tile_pool(name="x", bufs=BLOCKS))
             grouped_pool = head.enter_context(tc.tile_pool(name="grouped", bufs=3))
 
-            w_hh_rows = stage.tile([P, TILES, HID], BF16)
+            w_hh_rows = stage.tile([P, TILES, HID], BF16, align_bytes=DMA_ALIGN)
             nc.sync.dma_start(out=w_hh_rows[:], in_=w_hh.rearrange("(j p) k -> p j k", p=P))
             x_blocks = []
             block_cols = BLOCK_PASSES * K_PASS
             for m in range(BLOCKS):
-                x_block = x_pool.tile([P, block_cols], BF16)
+                x_block = x_pool.tile([P, block_cols], BF16, align_bytes=DMA_ALIGN)
                 nc.sync.dma_start(out=x_block[:], in_=x[:, m * block_cols : (m + 1) * block_cols])
                 x_blocks.append(x_block)
 
-            h_rows = stage.tile([P, HID], BF16)
+            h_rows = stage.tile([P, HID], BF16, align_bytes=DMA_ALIGN)
             nc.scalar.dma_start(out=h_rows[:], in_=h[:, :])
-            c_rows = stage.tile([P, HID], BF16)
+            c_rows = stage.tile([P, HID], BF16, align_bytes=DMA_ALIGN)
             nc.scalar.dma_start(out=c_rows[:], in_=c[:, :])
             for col, vector in (
                 (COL_B, b),
@@ -141,7 +138,7 @@ def tile_lstmcell_k_kernel(
                 load_scales(m)
 
             w_blocks = [
-                w_pool.tile([P, BLOCK_PASSES, GATES], U32, align_bytes=64, name="w_block", tag="w")
+                w_pool.tile([P, BLOCK_PASSES, GATES], U32, align_bytes=DMA_ALIGN, name="w_block", tag="w")
                 for m in range(BLOCKS)
             ]
 
@@ -374,12 +371,12 @@ def tile_lstmcell_k_kernel(
             )
         tanh_c = tail.tile([P, HID], F32)
         nc.scalar.copy(out=tanh_c[:], in_=to_rows(tanh_c_t, "acc0"))
-        c_next = tail.tile([P, HID], F32)
+        c_next = tail.tile([P, HID], F32, align_bytes=DMA_ALIGN)
         nc.scalar.copy(out=c_next[:], in_=to_rows(c_next_t, "acc1"))
         nc.sync.dma_start(out=out_0[:, :], in_=c_next[:])
 
         finish_gates(OUT_TILES, ACT.Sigmoid, "out")
-        h_next = tail.tile([P, HID], F32)
+        h_next = tail.tile([P, HID], F32, align_bytes=DMA_ALIGN)
         for s, bank_tag in enumerate(("acc2", "acc3")):
             bank = acc_pool.tile([P, P], F32, tag=bank_tag, name="rows_" + bank_tag)
             nc.tensor.transpose(bank[:], gate[:, OUT_TILES[s], :], ident_f32[:])

@@ -27,7 +27,7 @@ BLOCK_PASSES = 4
 BLOCKS = PASSES // BLOCK_PASSES
 LATE_BLOCKS = 6
 EARLY_BLOCKS = BLOCKS - LATE_BLOCKS
-FIRST_LOAD_PASSES = (1, 2)
+X_LOAD_BLOCKS = (1, 1, 2, 2, 2)
 VECTOR_SHARE = 3
 
 DMA_ALIGN = 256
@@ -95,17 +95,20 @@ def tile_lstmcell_k_kernel(
 
         with ExitStack() as head:
             stage = head.enter_context(tc.tile_pool(name="stage", bufs=1))
-            x_pool = head.enter_context(tc.tile_pool(name="x", bufs=BLOCKS))
+            x_pool = head.enter_context(tc.tile_pool(name="x", bufs=len(X_LOAD_BLOCKS)))
             grouped_pool = head.enter_context(tc.tile_pool(name="grouped", bufs=3))
 
             w_hh_rows = stage.tile([P, TILES, HID], BF16, align_bytes=DMA_ALIGN)
-            nc.sync.dma_start(out=w_hh_rows[:], in_=w_hh.rearrange("(j p) k -> p j k", p=P))
+            nc.sync.dma_start(out=w_hh_rows[:], in_=w_hh.rearrange("(p j) k -> p j k", p=P))
             x_blocks = []
             block_cols = BLOCK_PASSES * K_PASS
-            for m in range(BLOCKS):
-                x_block = x_pool.tile([P, block_cols], BF16, align_bytes=DMA_ALIGN)
-                nc.sync.dma_start(out=x_block[:], in_=x[:, m * block_cols : (m + 1) * block_cols])
-                x_blocks.append(x_block)
+            for load_blocks in X_LOAD_BLOCKS:
+                first_col = len(x_blocks) * block_cols
+                cols = load_blocks * block_cols
+                x_part = x_pool.tile([P, cols], BF16, align_bytes=DMA_ALIGN)
+                nc.sync.dma_start(out=x_part[:], in_=x[:, first_col : first_col + cols])
+                for part in range(load_blocks):
+                    x_blocks.append(x_part[:, part * block_cols : (part + 1) * block_cols])
 
             h_rows = stage.tile([P, HID], BF16, align_bytes=DMA_ALIGN)
             nc.scalar.dma_start(out=h_rows[:], in_=h[:, :])
@@ -142,20 +145,17 @@ def tile_lstmcell_k_kernel(
                 for m in range(BLOCKS)
             ]
 
-            def load_w(m, tiles, first_place=0, last_place=BLOCK_PASSES):
+            def load_w(m, tiles):
                 cols = slice(tiles[0] * P, (tiles[-1] + 1) * P)
-                first_pass = BLOCK_PASSES * m
                 nc.sync.dma_start(
-                    out=w_blocks[m][:, first_place:last_place, cols].bitcast(I32),
-                    in_=w_ih_words[first_pass + first_place : first_pass + last_place, :, cols, :]
+                    out=w_blocks[m][:, :, cols].bitcast(I32),
+                    in_=w_ih_words[BLOCK_PASSES * m : BLOCK_PASSES * (m + 1), :, cols, :]
                     .rearrange("g p n t -> p g (n t)")
                     .bitcast(I32),
                 )
 
             for m in range(EARLY_BLOCKS):
-                load_passes = FIRST_LOAD_PASSES[m]
-                for first_place in range(0, BLOCK_PASSES, load_passes):
-                    load_w(m, range(TILES), first_place, first_place + load_passes)
+                load_w(m, range(TILES))
             for late_tiles in (FORGET_IN_TILES, CELL_TILES, OUT_TILES):
                 for m in range(EARLY_BLOCKS, BLOCKS):
                     load_w(m, late_tiles)
@@ -187,7 +187,8 @@ def tile_lstmcell_k_kernel(
                         w_hh_bank[:, j, :], w_hh_rows[:, j, s * P : (s + 1) * P], ident_bf16[:]
                     )
                 nc.scalar.copy(
-                    out=w_hh_t[:, s, :].rearrange("p (j n) -> p j n", j=TILES), in_=w_hh_bank[:]
+                    out=w_hh_t[:, s, :].rearrange("p (n j) -> p n j", j=TILES),
+                    in_=w_hh_bank[:].rearrange("p j n -> p n j"),
                 )
             hh_part = keep.tile([P, TILES, BATCH], F32)
             tiles_per_bank = 4
@@ -238,7 +239,7 @@ def tile_lstmcell_k_kernel(
             x_planes = keep.tile([P, PASSES, BATCH], U8, align_bytes=64)
             passes_per_bank = 2
             for m in range(BLOCKS):
-                pairs = x_blocks[m][:].bitcast(F32)
+                pairs = x_blocks[m].bitcast(F32)
                 grouped = grouped_pool.tile([P, BLOCK_PASSES, BATCH, 4], BF16, align_bytes=64)
                 for first in range(0, BLOCK_PASSES, passes_per_bank):
                     x_bank = x_psum.tile([P, passes_per_bank, 2, BATCH], F32)

@@ -27,6 +27,7 @@ BLOCK_PASSES = 4
 BLOCKS = PASSES // BLOCK_PASSES
 LATE_BLOCKS = 6
 EARLY_BLOCKS = BLOCKS - LATE_BLOCKS
+SYNC_SCALE_BLOCK = BLOCKS - EARLY_BLOCKS
 X_LOAD_BLOCKS = (1, 1, 2, 2, 2)
 VECTOR_SHARE = 3
 
@@ -128,17 +129,17 @@ def tile_lstmcell_k_kernel(
                     out=vector_rows[col : col + rows, :], in_=vector.rearrange("(r e) -> r e", e=P)
                 )
 
-            def load_scales(m):
+            def load_scales(m, queue, view):
                 for quad in range(4):
-                    nc.gpsimd.dma_start(
-                        out=w_planes[32 * quad : 32 * quad + 16, m, :].bitcast(F32),
+                    queue.dma_start(
+                        out=w_planes[32 * quad : 32 * quad + 16, m, :].bitcast(view),
                         in_=w_ih_scales[
                             BLOCK_PASSES * m : BLOCK_PASSES * (m + 1), 4 * quad : 4 * quad + 4, :
-                        ].bitcast(F32),
+                        ].bitcast(view),
                     )
 
-            for m in range(BLOCKS):
-                load_scales(m)
+            for m in range(SYNC_SCALE_BLOCK):
+                load_scales(m, nc.gpsimd, F32)
 
             w_blocks = [
                 w_pool.tile([P, BLOCK_PASSES, GATES], U32, align_bytes=DMA_ALIGN, name="w_block", tag="w")
@@ -156,6 +157,7 @@ def tile_lstmcell_k_kernel(
 
             for m in range(EARLY_BLOCKS):
                 load_w(m, range(TILES))
+                load_scales(SYNC_SCALE_BLOCK + m, nc.sync, I32)
             for late_tiles in (FORGET_IN_TILES, CELL_TILES, OUT_TILES):
                 for m in range(EARLY_BLOCKS, BLOCKS):
                     load_w(m, late_tiles)

@@ -25,9 +25,7 @@ K_PASS = 512
 PASSES = IN // K_PASS
 BLOCK_PASSES = 4
 BLOCKS = PASSES // BLOCK_PASSES
-LATE_BLOCKS = 6
-EARLY_BLOCKS = BLOCKS - LATE_BLOCKS
-SYNC_SCALE_BLOCK = BLOCKS - EARLY_BLOCKS
+SYNC_SCALE_BLOCK = 6
 X_LOAD_BLOCKS = (1, 1, 2, 2, 2)
 VECTOR_SHARE = 3
 
@@ -38,6 +36,11 @@ HALVES = HID // P
 FORGET_IN_TILES = (0, 1, 2, 3)
 OUT_TILES = (4, 5)
 CELL_TILES = (6, 7)
+GROUP_LOADS = (
+    (FORGET_IN_TILES, (8, 8, 8, 4, 4)),
+    (CELL_TILES, (8, 8, 8, 4, 4)),
+    (OUT_TILES, (8, 8, 8, 4, 4)),
+)
 
 COL_B, COL_G_IH, COL_B_IH, COL_G_HH, COL_B_HH = 0, 8, 16, 24, 32
 COL_G_C, COL_B_C = 40, 42
@@ -73,7 +76,7 @@ def tile_lstmcell_k_kernel(
     nc = tc.nc
     with ExitStack() as whole:
         keep = whole.enter_context(tc.tile_pool(name="keep", bufs=1))
-        w_pool = whole.enter_context(tc.tile_pool(name="w_words", bufs=BLOCKS))
+        w_pool = whole.enter_context(tc.tile_pool(name="w_words", bufs=1))
 
         w_planes = keep.tile([P, BLOCKS, GATES], U8, align_bytes=DMA_ALIGN)
         for m in range(BLOCKS):
@@ -141,26 +144,27 @@ def tile_lstmcell_k_kernel(
             for m in range(SYNC_SCALE_BLOCK):
                 load_scales(m, nc.gpsimd, F32)
 
-            w_blocks = [
-                w_pool.tile([P, BLOCK_PASSES, GATES], U32, align_bytes=DMA_ALIGN, name="w_block", tag="w")
-                for m in range(BLOCKS)
-            ]
+            w_words = w_pool.tile([P, PASSES, GATES], U32, align_bytes=DMA_ALIGN)
 
-            def load_w(m, tiles):
+            def load_w(first_pass, count, tiles):
+                passes = slice(first_pass, first_pass + count)
                 cols = slice(tiles[0] * P, (tiles[-1] + 1) * P)
                 nc.sync.dma_start(
-                    out=w_blocks[m][:, :, cols].bitcast(I32),
-                    in_=w_ih_words[BLOCK_PASSES * m : BLOCK_PASSES * (m + 1), :, cols, :]
+                    out=w_words[:, passes, cols].bitcast(I32),
+                    in_=w_ih_words[passes, :, cols, :]
                     .rearrange("g p n t -> p g (n t)")
                     .bitcast(I32),
                 )
 
-            for m in range(EARLY_BLOCKS):
-                load_w(m, range(TILES))
-                load_scales(SYNC_SCALE_BLOCK + m, nc.sync, I32)
-            for late_tiles in (FORGET_IN_TILES, CELL_TILES, OUT_TILES):
-                for m in range(EARLY_BLOCKS, BLOCKS):
-                    load_w(m, late_tiles)
+            sync_scale_blocks = list(range(SYNC_SCALE_BLOCK, BLOCKS))
+            for group, load_passes in GROUP_LOADS:
+                first_pass = 0
+                for count in load_passes:
+                    load_w(first_pass, count, group)
+                    first_pass += count
+                    if sync_scale_blocks:
+                        load_scales(sync_scale_blocks[0], nc.sync, I32)
+                        sync_scale_blocks = sync_scale_blocks[1:]
 
             head_psum = head.enter_context(tc.psum_pool(name="head_psum", bufs=1))
             hh_psum = head.enter_context(tc.psum_pool(name="hh_psum", bufs=2))
@@ -277,7 +281,7 @@ def tile_lstmcell_k_kernel(
             cols = slice(j * P, (j + 1) * P)
             nc.tensor.matmul_mx(
                 out=acc[j][:],
-                lhsT=w_blocks[m][:, s, cols].bitcast(FP8X4),
+                lhsT=w_words[:, g, cols].bitcast(FP8X4),
                 lhsT_scale=w_planes[4 * s : P, m, cols],
                 rhs=x_words[:, g, :].bitcast(FP8X4),
                 rhs_scale=x_planes[:, g, :],
@@ -285,8 +289,8 @@ def tile_lstmcell_k_kernel(
                 stop=(g == PASSES - 1),
             )
 
-        def late_passes(tiles):
-            for g in range(EARLY_BLOCKS * BLOCK_PASSES, PASSES - BLOCK_PASSES):
+        def group_passes(tiles):
+            for g in range(PASSES - BLOCK_PASSES):
                 for j in tiles:
                     mx_pass(g, j)
             for j in tiles:
@@ -323,11 +327,8 @@ def tile_lstmcell_k_kernel(
                 nc.tensor.transpose(bank[:, s, :], result_t[:, s, :], ident_f32[:])
             return bank[:].rearrange("p s n -> p (s n)")
 
-        for g in range(EARLY_BLOCKS * BLOCK_PASSES):
-            for j in range(TILES):
-                mx_pass(g, j)
-        for late_tiles in (FORGET_IN_TILES, CELL_TILES, OUT_TILES):
-            late_passes(late_tiles)
+        for tiles in (FORGET_IN_TILES, CELL_TILES, OUT_TILES):
+            group_passes(tiles)
 
         finish_gates(FORGET_IN_TILES, ACT.Sigmoid, "forget_in")
         kept = tail.tile([P, HALVES, BATCH], F32)

from contextlib import ExitStack

import concourse.mybir as mybir
from concourse.masks import make_identity

F32 = mybir.dt.float32
BF16 = mybir.dt.bfloat16
I32 = mybir.dt.int32
U32 = mybir.dt.uint32
U8 = mybir.dt.uint8
FP8X4 = mybir.dt.float8_e4m3fn_x4
ALU = mybir.AluOpType
ACT = mybir.ActivationFunctionType

P = 128
BATCH = 128
IN = 16384
HID = 256
GATES = 4 * HID
EPS = 1e-5
TRIPLE = 3
STATS = 2 * TRIPLE

K_PASS = 512
PASSES = IN // K_PASS
BLOCK_PASSES = 4
BLOCKS = PASSES // BLOCK_PASSES
SYNC_SCALE_BLOCK = 6
X_LOAD_BLOCKS = (1, 1, 2, 2, 2)
VECTOR_SHARE = 3

DMA_ALIGN = 256

TILES = GATES // P
HALVES = HID // P
FORGET_IN_TILES = (0, 1, 2, 3)
OUT_TILES = (4, 5)
CELL_TILES = (6, 7)
GROUP_LOADS = (
    (FORGET_IN_TILES, (8, 8, 8, 4, 4)),
    (CELL_TILES, (8, 8, 8, 4, 4)),
    (OUT_TILES, (8, 8, 8, 4, 4)),
)

COL_B, COL_G_IH, COL_B_IH, COL_G_HH, COL_B_HH = 0, 8, 16, 24, 32
COL_G_C, COL_B_C = 40, 42
VECTOR_COLS = 44

FLOPS = 2 * BATCH * IN * GATES + 2 * BATCH * HID * GATES


def centre_and_rstd(nc, pool, neg_half, stats, sources, gains, centred, label):
    count = len(sources)
    mean_var = pool.tile([P, count, 2], F32, name=label + "_mean_var")
    for t in range(count):
        nc.vector.bn_stats(out=stats[:, t, 0:STATS], in_=sources[t])
    for t in range(count):
        nc.vector.bn_aggr(out=mean_var[:, t, :], in_=stats[:, t, :])
    rstd = pool.tile([P, count], F32, name=label + "_rstd")
    nc.gpsimd.tensor_tensor(out=rstd[:], in0=mean_var[:, :, 1], in1=neg_half[:, 0:count], op=ALU.pow)
    for t in range(count):
        nc.vector.tensor_scalar(
            out=centred[t],
            in0=sources[t],
            scalar1=mean_var[:, t, 0:1],
            scalar2=gains[t],
            op0=ALU.subtract,
            op1=ALU.mult,
        )
    return rstd


def tile_lstmcell_k_kernel(
    tc, x, c, h, w_ih_words, w_ih_scales, w_hh, b, g_ih, b_ih, g_hh, b_hh, g_c, b_c, out_0, out_1
):
    nc = tc.nc
    with ExitStack() as whole:
        keep = whole.enter_context(tc.tile_pool(name="keep", bufs=1))
        w_pool = whole.enter_context(tc.tile_pool(name="w_words", bufs=1))

        w_planes = keep.tile([P, BLOCKS, GATES], U8, align_bytes=DMA_ALIGN)
        for m in range(BLOCKS):
            nc.vector.memset(w_planes[:, m, :].bitcast(I32), 0)
        vector_rows = keep.tile([P, P], BF16, align_bytes=DMA_ALIGN)
        nc.vector.memset(vector_rows[:], 0.0)
        neg_half = keep.tile([P, TILES], F32)
        nc.vector.memset(neg_half[:], -0.5)
        stats = keep.tile([P, 2 * TILES + HALVES, STATS + TRIPLE], F32)
        nc.vector.memset(stats[:, :, STATS:], 0.0)
        nc.vector.memset(stats[:, :, STATS + TRIPLE - 1 :], BATCH * EPS)
        ident_f32 = keep.tile([P, P], F32)
        make_identity(nc, ident_f32[:])
        ident_bf16 = keep.tile([P, P], BF16)
        nc.vector.tensor_copy(out=ident_bf16[:], in_=ident_f32[:])
        table_in = keep.tile([P, 1], F32)
        nc.vector.memset(table_in[:], 0.0)
        table_out = keep.tile([P, 1], F32)
        nc.scalar.activation(out=table_out[:], in_=table_in[:], func=ACT.Sigmoid)

        with ExitStack() as head:
            stage = head.enter_context(tc.tile_pool(name="stage", bufs=1))
            x_pool = head.enter_context(tc.tile_pool(name="x", bufs=len(X_LOAD_BLOCKS)))
            grouped_pool = head.enter_context(tc.tile_pool(name="grouped", bufs=3))

            w_hh_rows = stage.tile([P, TILES, HID], BF16, align_bytes=DMA_ALIGN)
            nc.sync.dma_start(out=w_hh_rows[:], in_=w_hh.rearrange("(p j) k -> p j k", p=P))
            x_blocks = []
            block_cols = BLOCK_PASSES * K_PASS
            for load_blocks in X_LOAD_BLOCKS:
                first_col = len(x_blocks) * block_cols
                cols = load_blocks * block_cols
                x_part = x_pool.tile([P, cols], BF16, align_bytes=DMA_ALIGN)
                nc.sync.dma_start(out=x_part[:], in_=x[:, first_col : first_col + cols])
                for part in range(load_blocks):
                    x_blocks.append(x_part[:, part * block_cols : (part + 1) * block_cols])

            h_rows = stage.tile([P, HID], BF16, align_bytes=DMA_ALIGN)
            nc.scalar.dma_start(out=h_rows[:], in_=h[:, :])
            c_rows = stage.tile([P, HID], BF16, align_bytes=DMA_ALIGN)
            nc.scalar.dma_start(out=c_rows[:], in_=c[:, :])
            for col, vector in (
                (COL_B, b),
                (COL_G_IH, g_ih),
                (COL_B_IH, b_ih),
                (COL_G_HH, g_hh),
                (COL_B_HH, b_hh),
                (COL_G_C, g_c),
                (COL_B_C, b_c),
            ):
                rows = vector.shape[0] // P
                nc.scalar.dma_start(
                    out=vector_rows[col : col + rows, :], in_=vector.rearrange("(r e) -> r e", e=P)
                )

            def load_scales(m, queue, view):
                for quad in range(4):
                    queue.dma_start(
                        out=w_planes[32 * quad : 32 * quad + 16, m, :].bitcast(view),
                        in_=w_ih_scales[
                            BLOCK_PASSES * m : BLOCK_PASSES * (m + 1), 4 * quad : 4 * quad + 4, :
                        ].bitcast(view),
                    )

            for m in range(SYNC_SCALE_BLOCK):
                load_scales(m, nc.gpsimd, F32)

            w_words = w_pool.tile([P, PASSES, GATES], U32, align_bytes=DMA_ALIGN)

            def load_w(first_pass, count, tiles):
                passes = slice(first_pass, first_pass + count)
                cols = slice(tiles[0] * P, (tiles[-1] + 1) * P)
                nc.sync.dma_start(
                    out=w_words[:, passes, cols].bitcast(I32),
                    in_=w_ih_words[passes, :, cols, :]
                    .rearrange("g p n t -> p g (n t)")
                    .bitcast(I32),
                )

            sync_scale_blocks = list(range(SYNC_SCALE_BLOCK, BLOCKS))
            for group, load_passes in GROUP_LOADS:
                first_pass = 0
                for count in load_passes:
                    load_w(first_pass, count, group)
                    first_pass += count
                    if sync_scale_blocks:
                        load_scales(sync_scale_blocks[0], nc.sync, I32)
                        sync_scale_blocks = sync_scale_blocks[1:]

            head_psum = head.enter_context(tc.psum_pool(name="head_psum", bufs=1))
            hh_psum = head.enter_context(tc.psum_pool(name="hh_psum", bufs=2))
            x_psum = head.enter_context(tc.psum_pool(name="x_psum", bufs=4))

            small_t = head_psum.tile([P, 2 * HALVES + 1, P], BF16)
            h_t = stage.tile([P, HALVES, BATCH], BF16)
            c_t = keep.tile([P, HALVES, BATCH], BF16)
            vectors = keep.tile([P, VECTOR_COLS], F32)
            for s in range(HALVES):
                nc.tensor.transpose(small_t[:, s, :], h_rows[:, s * P : (s + 1) * P], ident_bf16[:])
            nc.vector.tensor_copy(out=h_t[:], in_=small_t[:, 0:HALVES, :])
            for s in range(HALVES):
                nc.tensor.transpose(
                    small_t[:, HALVES + s, :], c_rows[:, s * P : (s + 1) * P], ident_bf16[:]
                )
            nc.vector.tensor_copy(out=c_t[:], in_=small_t[:, HALVES : 2 * HALVES, :])
            nc.tensor.transpose(small_t[:, 2 * HALVES, :], vector_rows[:], ident_bf16[:])
            nc.vector.tensor_copy(out=vectors[:], in_=small_t[:, 2 * HALVES, 0:VECTOR_COLS])

            w_hh_t = stage.tile([P, HALVES, GATES], BF16)
            for s in range(HALVES):
                w_hh_bank = hh_psum.tile([P, TILES, P], BF16, tag="hh")
                for j in range(TILES):
                    nc.tensor.transpose(
                        w_hh_bank[:, j, :], w_hh_rows[:, j, s * P : (s + 1) * P], ident_bf16[:]
                    )
                nc.scalar.copy(
                    out=w_hh_t[:, s, :].rearrange("p (n j) -> p n j", j=TILES),
                    in_=w_hh_bank[:].rearrange("p j n -> p n j"),
                )
            hh_part = keep.tile([P, TILES, BATCH], F32)
            tiles_per_bank = 4
            for bank in range(TILES // tiles_per_bank):
                hh_bank = hh_psum.tile([P, tiles_per_bank, BATCH], F32, tag="hh")
                for t in range(tiles_per_bank):
                    j = bank * tiles_per_bank + t
                    for s in range(HALVES):
                        nc.tensor.matmul(
                            hh_bank[:, t, :],
                            lhsT=w_hh_t[:, s, j * P : (j + 1) * P],
                            rhs=h_t[:, s, :],
                            start=(s == 0),
                            stop=(s == HALVES - 1),
                        )
                bank_tiles = slice(bank * tiles_per_bank, (bank + 1) * tiles_per_bank)
                nc.scalar.copy(out=hh_part[:, bank_tiles, :], in_=hh_bank[:])
            bias_sum = stage.tile([P, TILES], F32)
            nc.vector.tensor_add(
                out=bias_sum[:],
                in0=vectors[:, COL_B : COL_B + TILES],
                in1=vectors[:, COL_B_IH : COL_B_IH + TILES],
            )
            nc.vector.tensor_add(
                out=bias_sum[:], in0=bias_sum[:], in1=vectors[:, COL_B_HH : COL_B_HH + TILES]
            )
            hh_tiles = [hh_part[:, j, :] for j in range(TILES)]
            hh_rstd = centre_and_rstd(
                nc,
                stage,
                neg_half,
                stats[:, 0:TILES, :],
                hh_tiles,
                [vectors[:, COL_G_HH + j : COL_G_HH + j + 1] for j in range(TILES)],
                hh_tiles,
                "hh",
            )
            for j in range(TILES):
                nc.scalar.activation(
                    out=hh_part[:, j, :],
                    in_=hh_part[:, j, :],
                    func=ACT.Identity,
                    scale=hh_rstd[:, j : j + 1],
                    bias=bias_sum[:, j : j + 1],
                )

            x_words = keep.tile([P, PASSES, BATCH], U32, align_bytes=64)
            x_planes = keep.tile([P, PASSES, BATCH], U8, align_bytes=64)
            passes_per_bank = 2
            for m in range(BLOCKS):
                pairs = x_blocks[m].bitcast(F32)
                grouped = grouped_pool.tile([P, BLOCK_PASSES, BATCH, 4], BF16, align_bytes=64)
                for first in range(0, BLOCK_PASSES, passes_per_bank):
                    x_bank = x_psum.tile([P, passes_per_bank, 2, BATCH], F32)
                    for r in range(passes_per_bank):
                        first_word = (first + r) * (K_PASS // 2)
                        for u in range(2):
                            nc.tensor.transpose(
                                x_bank[:, r, u, :],
                                pairs[:, first_word + u : first_word + K_PASS // 2 : 2],
                                ident_f32[:],
                            )
                    bank_index = (m * BLOCK_PASSES + first) // passes_per_bank
                    words_out = grouped[:].bitcast(F32)[:, first : first + passes_per_bank, :, :]
                    words_in = x_bank[:].rearrange("p r u b -> p r b u")
                    if bank_index % VECTOR_SHARE == VECTOR_SHARE - 1:
                        nc.vector.tensor_copy(out=words_out, in_=words_in)
                    else:
                        nc.scalar.copy(out=words_out, in_=words_in)
                block = slice(m * BLOCK_PASSES, (m + 1) * BLOCK_PASSES)
                nc.vector.quantize_mx(
                    out=x_words[:, block, :].rearrange("p g b -> p (g b)").bitcast(FP8X4),
                    scales=x_planes[:, block, :].rearrange("p g b -> p (g b)"),
                    in_=grouped[:].rearrange("p g b t -> p (g b t)"),
                )

        whole.enter_context(tc.manual_schedule())
        acc_pool = whole.enter_context(tc.psum_pool(name="acc", bufs=1))
        tail = whole.enter_context(tc.tile_pool(name="tail", bufs=1))
        acc = [acc_pool.tile([P, BATCH], F32, name="acc%d" % j) for j in range(TILES)]

        def mx_pass(g, j):
            m, s = divmod(g, BLOCK_PASSES)
            cols = slice(j * P, (j + 1) * P)
            nc.tensor.matmul_mx(
                out=acc[j][:],
                lhsT=w_words[:, g, cols].bitcast(FP8X4),
                lhsT_scale=w_planes[4 * s : P, m, cols],
                rhs=x_words[:, g, :].bitcast(FP8X4),
                rhs_scale=x_planes[:, g, :],
                start=(g == 0),
                stop=(g == PASSES - 1),
            )

        def group_passes(tiles):
            for g in range(PASSES - BLOCK_PASSES):
                for j in tiles:
                    mx_pass(g, j)
            for j in tiles:
                for g in range(PASSES - BLOCK_PASSES, PASSES):
                    mx_pass(g, j)

        gate = tail.tile([P, TILES, BATCH], F32)

        def finish_gates(tiles, func, label):
            rstd = centre_and_rstd(
                nc,
                tail,
                neg_half,
                stats[:, TILES + tiles[0] : TILES + tiles[-1] + 1, :],
                [acc[j][:] for j in tiles],
                [vectors[:, COL_G_IH + j : COL_G_IH + j + 1] for j in tiles],
                [gate[:, j, :] for j in tiles],
                label,
            )
            for t, j in enumerate(tiles):
                nc.vector.scalar_tensor_tensor(
                    out=gate[:, j, :],
                    in0=gate[:, j, :],
                    scalar=rstd[:, t : t + 1],
                    in1=hh_part[:, j, :],
                    op0=ALU.mult,
                    op1=ALU.add,
                )
                nc.scalar.activation(out=gate[:, j, :], in_=gate[:, j, :], func=func)

        def to_rows(result_t, bank_tag):
            bank = acc_pool.tile([P, HALVES, P], F32, tag=bank_tag, name="rows_" + bank_tag)
            for s in range(HALVES):
                nc.tensor.transpose(bank[:, s, :], result_t[:, s, :], ident_f32[:])
            return bank[:].rearrange("p s n -> p (s n)")

        for tiles in (FORGET_IN_TILES, CELL_TILES, OUT_TILES):
            group_passes(tiles)

        finish_gates(FORGET_IN_TILES, ACT.Sigmoid, "forget_in")
        kept = tail.tile([P, HALVES, BATCH], F32)
        nc.vector.tensor_mul(out=kept[:], in0=gate[:, 0:HALVES, :], in1=c_t[:])
        finish_gates(CELL_TILES, ACT.Tanh, "cell")
        added = tail.tile([P, HALVES, BATCH], F32)
        for s in range(HALVES):
            nc.vector.tensor_mul(
                out=added[:, s, :],
                in0=gate[:, HALVES + s, :],
                in1=gate[:, CELL_TILES[s], :],
            )
        c_raw = tail.tile([P, HALVES, BATCH], F32)
        for s in range(HALVES):
            nc.vector.tensor_add(out=c_raw[:, s, :], in0=kept[:, s, :], in1=added[:, s, :])
        c_centred = tail.tile([P, HALVES, BATCH], F32)
        c_rstd = centre_and_rstd(
            nc,
            tail,
            neg_half,
            stats[:, 2 * TILES : 2 * TILES + HALVES, :],
            [c_raw[:, s, :] for s in range(HALVES)],
            [vectors[:, COL_G_C + s : COL_G_C + s + 1] for s in range(HALVES)],
            [c_centred[:, s, :] for s in range(HALVES)],
            "c",
        )
        c_next_t = tail.tile([P, HALVES, BATCH], F32)
        tanh_c_t = tail.tile([P, HALVES, BATCH], F32)
        for s in range(HALVES):
            nc.scalar.activation(
                out=tanh_c_t[:, s, :],
                in_=c_centred[:, s, :],
                func=ACT.Tanh,
                scale=c_rstd[:, s : s + 1],
                bias=vectors[:, COL_B_C + s : COL_B_C + s + 1],
            )
            nc.vector.tensor_scalar(
                out=c_next_t[:, s, :],
                in0=c_centred[:, s, :],
                scalar1=c_rstd[:, s : s + 1],
                scalar2=vectors[:, COL_B_C + s : COL_B_C + s + 1],
                op0=ALU.mult,
                op1=ALU.add,
            )
        tanh_c = tail.tile([P, HID], F32)
        nc.scalar.copy(out=tanh_c[:], in_=to_rows(tanh_c_t, "acc0"))
        c_next = tail.tile([P, HID], F32, align_bytes=DMA_ALIGN)
        nc.scalar.copy(out=c_next[:], in_=to_rows(c_next_t, "acc1"))
        nc.sync.dma_start(out=out_0[:, :], in_=c_next[:])

        finish_gates(OUT_TILES, ACT.Sigmoid, "out")
        h_next = tail.tile([P, HID], F32, align_bytes=DMA_ALIGN)
        for s, bank_tag in enumerate(("acc2", "acc3")):
            bank = acc_pool.tile([P, P], F32, tag=bank_tag, name="rows_" + bank_tag)
            nc.tensor.transpose(bank[:], gate[:, OUT_TILES[s], :], ident_f32[:])
            cols = slice(s * P, (s + 1) * P)
            nc.vector.tensor_mul(out=h_next[:, cols], in0=bank[:], in1=tanh_c[:, cols])
        nc.sync.dma_start(out=out_1[:, :], in_=h_next[:])
